import numpy as np
import ml_dtypes


def mxq(x, axis, fmt="e4m3"):
    dtype, down = {"e4m3": (ml_dtypes.float8_e4m3fn, 7), "e5m2": (ml_dtypes.float8_e5m2, 14)}[fmt]
    v = np.moveaxis(np.asarray(x, np.float32).astype(ml_dtypes.bfloat16).astype(np.float64), axis, -1)
    blocks = v.reshape(v.shape[:-1] + (-1, 32))
    amax = np.abs(blocks).max(-1, keepdims=True)
    byte = np.maximum(np.where(amax > 0, np.frexp(amax)[1] - 1 + 127, 0) - down, 1)
    scale = np.exp2(byte - 127.0)
    codes = (blocks / scale).astype(np.float32).astype(dtype).astype(np.float64)
    return np.moveaxis((codes * scale).reshape(v.shape), -1, axis)


WIDE = False


def mx_kscale(k):
    if not WIDE:
        return np.ones(k)
    levels = np.array([10, -10, 5, -5, 0])
    if k % 512:
        return np.exp2(np.random.permutation(np.resize(levels, k // 32))).repeat(32)
    a = np.empty((k // 512, 16))
    for p in range(k // 512):
        a[p, :8] = np.random.permutation(np.resize(levels, 8))
        for g in range(8):
            far = levels[np.abs(levels - a[p, g]) >= 10]
            a[p, g + 8] = far[np.random.randint(len(far))]
    return np.exp2(a.ravel()).repeat(32)


BF16 = ml_dtypes.bfloat16


def bf(x):
    return np.asarray(x, np.float32).astype(BF16)


def f64(x):
    return np.asarray(x).astype(np.float64)


B, I, C, L, O, KW, P = 1, 512, 4, 128, 128, 3, 1


def setup_inputs():
    s = mx_kscale(I)
    return {"x": bf(np.random.standard_normal((B, I, C, L)) * s[None, :, None, None]),
            "time_tensor": bf(np.random.uniform(0.0, 1.0, (B, C, L))),
            "weights": bf(np.random.standard_normal((O, I, C, KW)) / np.sqrt(I * KW) / s[None, :, None, None])}


def reference(x, time_tensor, weights):
    xq = mxq(f64(x).transpose(0, 2, 1, 3), 2, "e4m3")
    wt = f64(weights).transpose(3, 2, 0, 1)
    tp = np.pad(f64(time_tensor), ((0, 0), (0, 0), (P, P)))
    Lw = L + 2 * P - KW + 1
    conv = np.zeros((B, C, O, Lw))
    for j in range(KW):
        y = mxq(wt[j], 2, "e4m3") @ xq
        conv = conv + np.pad(y, ((0, 0), (0, 0), (0, 0), (P, P)))[..., j:j + Lw]
    conv = np.transpose(conv, (0, 2, 1, 3))
    conv = np.pad(conv, ((0, 0), (0, 0), (0, 0), (P, P)))
    out = conv * tp[:, None, :, :]
    return out[..., P:-P]

@@ -1,0 +1,137 @@
+from contextlib import ExitStack
+
+import concourse.mybir as mybir
+from concourse.masks import make_identity
+
+BF16 = mybir.dt.bfloat16
+F32 = mybir.dt.float32
+U32 = mybir.dt.uint32
+U8 = mybir.dt.uint8
+FP8X4 = mybir.dt.float8_e4m3fn_x4
+
+P = 128
+PACK = 4
+I, C, L, O, KW = 512, 4, 128, 128, 3
+CK = C * KW
+PAIRS = CK // 2
+HALF = L // 2
+BLOCKS = KW + 1
+ROUND = 3
+
+FLOPS = 2 * O * I * C * KW * L
+
+
+def tile_timeawareconv1d_s_kernel(tc, x, time_tensor, weights, out):
+    nc = tc.nc
+    assert I == P * PACK and O == P
+
+    x_rows = x.rearrange("b (p t) c l -> p (b t) (c l)", p=P)
+    w_rows = weights.rearrange("o (t i) c k -> t o (i c k)", t=PACK)
+    time_row = time_tensor.rearrange("b c l -> b (c l)")
+    out_rows = out.rearrange("b o c l -> o (b c) l")
+
+    with ExitStack() as ctx:
+        keep = ctx.enter_context(tc.tile_pool(name="keep", bufs=1))
+        psum_w = ctx.enter_context(tc.psum_pool(name="psum_w", bufs=PAIRS))
+        psum_acc = ctx.enter_context(tc.psum_pool(name="psum_acc", bufs=2))
+
+        identity = keep.tile([P, P], F32)
+        make_identity(nc, identity[:])
+
+        ones = keep.tile([P, P], BF16)
+        nc.vector.memset(ones[:], 1.0)
+        time_in_row0 = keep.tile([P, C * L], BF16)
+        nc.vector.memset(time_in_row0[:], 0.0)
+        nc.scalar.dma_start(out=time_in_row0[0:1, :], in_=time_row)
+
+        w_raw = keep.tile([P, I, CK], BF16)
+        x_raw = keep.tile([P, PACK, C, L], BF16)
+        for t in range(PACK):
+            nc.sync.dma_start(out=w_raw[:, t * P : (t + 1) * P, :].rearrange("o i q -> o (i q)"), in_=w_rows[t])
+            if t == 1:
+                nc.sync.dma_start(out=x_raw[:].rearrange("p t c l -> p t (c l)"), in_=x_rows)
+
+        w_banks = [psum_w.tile([P, PACK, O], F32, name="w_bank%d" % w, tag="w_bank") for w in range(PAIRS)]
+        time_all = keep.tile([P, C, L], F32)
+        for half in range(2):
+            for w in range(PAIRS):
+                for t in (2 * half, 2 * half + 1):
+                    nc.tensor.transpose(w_banks[w][:, t, :], w_raw[:].bitcast(F32)[:, t::PACK, w], identity[:])
+            if half == 0:
+                time_bank = psum_acc.tile([P, C, L], F32, tag="acc")
+                nc.tensor.matmul(
+                    out=time_bank[:].rearrange("p c l -> p (c l)"),
+                    lhsT=ones[:],
+                    rhs=time_in_row0[:],
+                    start=True,
+                    stop=True,
+                )
+                nc.scalar.copy(out=time_all[:], in_=time_bank[:])
+
+        x_grouped = keep.tile([P, C, BLOCKS, HALF, PACK], BF16, align_bytes=64)
+        x_codes = keep.tile([P, C, BLOCKS * HALF], U32, align_bytes=64)
+        x_scales = keep.tile([P, C, BLOCKS * HALF], U8, align_bytes=64)
+        x_by_parity = x_raw[:].rearrange("p t c (n e) -> p e c n t", e=2)
+        nc.vector.tensor_copy(out=x_grouped[:, :, 1, :, :], in_=x_by_parity[:, 0])
+        nc.vector.tensor_copy(out=x_grouped[:, :, 2, :, :], in_=x_by_parity[:, 1])
+        nc.vector.memset(x_grouped[:, :, 0, 0, :], 0.0)
+        nc.vector.tensor_copy(out=x_grouped[:, :, 0, 1:HALF, :], in_=x_grouped[:, :, 2, 0 : HALF - 1, :])
+        nc.vector.tensor_copy(out=x_grouped[:, :, 3, 0 : HALF - 1, :], in_=x_grouped[:, :, 1, 1:HALF, :])
+        nc.vector.memset(x_grouped[:, :, 3, HALF - 1, :], 0.0)
+        nc.vector.quantize_mx(
+            out=x_codes[:].rearrange("p c w -> p (c w)").bitcast(FP8X4),
+            scales=x_scales[:].rearrange("p c w -> p (c w)"),
+            in_=x_grouped[:].rearrange("p c s n t -> p (c s n t)"),
+        )
+
+        w_grouped = keep.tile([P, CK, O, PACK], BF16, align_bytes=64)
+        w_codes = keep.tile([P, CK, O], U32, align_bytes=64)
+        w_scales = keep.tile([P, CK, O], U8, align_bytes=64)
+        out_sb = keep.tile([P, C, L], F32)
+
+        def copy_out(r):
+            for w in (r * ROUND + 2, r * ROUND, r * ROUND + 1):
+                engine_copy = nc.vector.tensor_copy if w % ROUND == 2 else nc.scalar.copy
+                engine_copy(
+                    out=w_grouped[:, 2 * w : 2 * w + 2, :, :],
+                    in_=w_banks[w][:].bitcast(BF16).rearrange("p t (o e) -> p e o t", e=2),
+                )
+
+        def quantise(r):
+            for w in range(r * ROUND, (r + 1) * ROUND):
+                both = slice(2 * w, 2 * w + 2)
+                nc.vector.quantize_mx(
+                    out=w_codes[:, both, :].rearrange("p q o -> p (q o)").bitcast(FP8X4),
+                    scales=w_scales[:, both, :].rearrange("p q o -> p (q o)"),
+                    in_=w_grouped[:, both, :, :].rearrange("p q o t -> p (q o t)"),
+                )
+
+        def finish(r):
+            channels = slice(2 * r, 2 * r + 2)
+            acc = psum_acc.tile([P, 2, L], F32, tag="acc")
+            for c in (2 * r, 2 * r + 1):
+                for k in range(KW):
+                    window = slice(k * HALF, k * HALF + L)
+                    nc.tensor.matmul_mx(
+                        out=acc[:, c % 2, :],
+                        lhsT=w_codes[:, c * KW + k, :].bitcast(FP8X4),
+                        lhsT_scale=w_scales[:, c * KW + k, :],
+                        rhs=x_codes[:, c, window].bitcast(FP8X4),
+                        rhs_scale=x_scales[:, c, window],
+                        start=(k == 0),
+                        stop=(k == KW - 1),
+                    )
+            nc.vector.tensor_tensor(
+                out=out_sb[:, channels, :].rearrange("p c (n e) -> p c n e", e=2),
+                in0=acc[:].rearrange("p c (e n) -> p c n e", e=2),
+                in1=time_all[:, channels, :].rearrange("p c (n e) -> p c n e", e=2),
+                op=mybir.AluOpType.mult,
+            )
+            nc.sync.dma_start(out=out_rows[:, channels, :], in_=out_sb[:, channels, :])
+
+        copy_out(0)
+        quantise(0)
+        copy_out(1)
+        finish(0)
+        quantise(1)
+        finish(1)

@@ -16,68 +16,71 @@ CK = C * KW
 PAIRS = CK // 2
 HALF = L // 2
 BLOCKS = KW + 1
-ROUND = 3
+B32 = I // 32
+OH = O // 2
 
 FLOPS = 2 * O * I * C * KW * L
 
 
 def tile_timeawareconv1d_s_kernel(tc, x, time_tensor, weights, out):
     nc = tc.nc
-    assert I == P * PACK and O == P
 
-    x_rows = x.rearrange("b (p t) c l -> p (b t) (c l)", p=P)
-    w_rows = weights.rearrange("o (t i) c k -> t o (i c k)", t=PACK)
+    x_rows = x.rearrange("a (b s r u) c l -> (a s) b r (u c l)", b=B32, s=2, r=8, u=2)
+    w_rows = weights.rearrange("(n o) (b s j) c k -> n s o b (j c k)", n=2, b=B32, s=2)
     time_row = time_tensor.rearrange("b c l -> b (c l)")
     out_rows = out.rearrange("b o c l -> o (b c) l")
 
     with ExitStack() as ctx:
         keep = ctx.enter_context(tc.tile_pool(name="keep", bufs=1))
-        psum_w = ctx.enter_context(tc.psum_pool(name="psum_w", bufs=PAIRS))
+        psum_w = ctx.enter_context(tc.psum_pool(name="psum_w", bufs=6))
         psum_acc = ctx.enter_context(tc.psum_pool(name="psum_acc", bufs=2))
+        ctx.enter_context(tc.manual_schedule())
 
-        identity = keep.tile([P, P], F32)
-        make_identity(nc, identity[:])
+        time_in_row0 = keep.tile([P, C * L], BF16)
+        nc.vector.memset(time_in_row0[:].bitcast(F32), 0.0)
+        nc.scalar.dma_start(out=time_in_row0[0:1, :], in_=time_row)
+
+        x_raw = keep.tile([P, 2, 2, C, L], BF16)
+        w_raw = [keep.tile([P, B32 * 16, CK], BF16, name="w_raw%d" % n) for n in range(2)]
+        for s in range(2):
+            nc.sync.dma_start(
+                out=x_raw[:, s].rearrange("p u c l -> p (u c l)"),
+                in_=x_rows[s],
+            )
+        for n in range(2):
+            for s in range(2):
+                nc.sync.dma_start(
+                    out=w_raw[n][s::2].rearrange("o (b j) q -> o b (j q)", b=B32),
+                    in_=w_rows[n, s],
+                )
 
         ones = keep.tile([P, P], BF16)
         nc.vector.memset(ones[:], 1.0)
-        time_in_row0 = keep.tile([P, C * L], BF16)
-        nc.vector.memset(time_in_row0[:], 0.0)
-        nc.scalar.dma_start(out=time_in_row0[0:1, :], in_=time_row)
-
-        w_raw = keep.tile([P, I, CK], BF16)
-        x_raw = keep.tile([P, PACK, C, L], BF16)
-        for t in range(PACK):
-            nc.sync.dma_start(out=w_raw[:, t * P : (t + 1) * P, :].rearrange("o i q -> o (i q)"), in_=w_rows[t])
-            if t == 1:
-                nc.sync.dma_start(out=x_raw[:].rearrange("p t c l -> p t (c l)"), in_=x_rows)
-
-        w_banks = [psum_w.tile([P, PACK, O], F32, name="w_bank%d" % w, tag="w_bank") for w in range(PAIRS)]
-        time_all = keep.tile([P, C, L], F32)
-        for half in range(2):
-            for w in range(PAIRS):
-                for t in (2 * half, 2 * half + 1):
-                    nc.tensor.transpose(w_banks[w][:, t, :], w_raw[:].bitcast(F32)[:, t::PACK, w], identity[:])
-            if half == 0:
-                time_bank = psum_acc.tile([P, C, L], F32, tag="acc")
-                nc.tensor.matmul(
-                    out=time_bank[:].rearrange("p c l -> p (c l)"),
-                    lhsT=ones[:],
-                    rhs=time_in_row0[:],
-                    start=True,
-                    stop=True,
-                )
-                nc.scalar.copy(out=time_all[:], in_=time_bank[:])
 
         x_grouped = keep.tile([P, C, BLOCKS, HALF, PACK], BF16, align_bytes=64)
         x_codes = keep.tile([P, C, BLOCKS * HALF], U32, align_bytes=64)
         x_scales = keep.tile([P, C, BLOCKS * HALF], U8, align_bytes=64)
-        x_by_parity = x_raw[:].rearrange("p t c (n e) -> p e c n t", e=2)
-        nc.vector.tensor_copy(out=x_grouped[:, :, 1, :, :], in_=x_by_parity[:, 0])
-        nc.vector.tensor_copy(out=x_grouped[:, :, 2, :, :], in_=x_by_parity[:, 1])
         nc.vector.memset(x_grouped[:, :, 0, 0, :], 0.0)
-        nc.vector.tensor_copy(out=x_grouped[:, :, 0, 1:HALF, :], in_=x_grouped[:, :, 2, 0 : HALF - 1, :])
-        nc.vector.tensor_copy(out=x_grouped[:, :, 3, 0 : HALF - 1, :], in_=x_grouped[:, :, 1, 1:HALF, :])
         nc.vector.memset(x_grouped[:, :, 3, HALF - 1, :], 0.0)
+
+        identity = keep.tile([P, P], F32)
+        make_identity(nc, identity[:])
+        parted = keep.tile([P, 2, OH], F32)
+        nc.vector.tensor_copy(out=parted[:], in_=identity[:].rearrange("p (o s) -> p s o", s=2))
+
+        time_all = keep.tile([P, C, L], F32)
+        time_bank = psum_acc.tile([P, C, L], F32, tag="acc")
+        nc.tensor.matmul(
+            out=time_bank[:].rearrange("p c l -> p (c l)"), lhsT=ones[:], rhs=time_in_row0[:], start=True, stop=True
+        )
+
+        x_by_parity = x_raw[:].rearrange("p s u c (n e) -> p e c n u s", e=2)
+        for blk in (1, 2):
+            nc.vector.tensor_copy(
+                out=x_grouped[:, :, blk, :, :].rearrange("p c n (u s) -> p c n u s", s=2), in_=x_by_parity[:, blk - 1]
+            )
+        nc.scalar.copy(out=x_grouped[:, :, 3, 0 : HALF - 1, :], in_=x_grouped[:, :, 1, 1:HALF, :])
+        nc.vector.tensor_copy(out=x_grouped[:, :, 0, 1:HALF, :], in_=x_grouped[:, :, 2, 0 : HALF - 1, :])
         nc.vector.quantize_mx(
             out=x_codes[:].rearrange("p c w -> p (c w)").bitcast(FP8X4),
             scales=x_scales[:].rearrange("p c w -> p (c w)"),
@@ -89,25 +92,33 @@ def tile_timeawareconv1d_s_kernel(tc, x, time_tensor, weights, out):
         w_scales = keep.tile([P, CK, O], U8, align_bytes=64)
         out_sb = keep.tile([P, C, L], F32)
 
-        def copy_out(r):
-            for w in (r * ROUND + 2, r * ROUND, r * ROUND + 1):
-                engine_copy = nc.vector.tensor_copy if w % ROUND == 2 else nc.scalar.copy
-                engine_copy(
-                    out=w_grouped[:, 2 * w : 2 * w + 2, :, :],
-                    in_=w_banks[w][:].bitcast(BF16).rearrange("p t (o e) -> p e o t", e=2),
-                )
+        banks = {}
 
-        def quantise(r):
-            for w in range(r * ROUND, (r + 1) * ROUND):
-                both = slice(2 * w, 2 * w + 2)
-                nc.vector.quantize_mx(
-                    out=w_codes[:, both, :].rearrange("p q o -> p (q o)").bitcast(FP8X4),
-                    scales=w_scales[:, both, :].rearrange("p q o -> p (q o)"),
-                    in_=w_grouped[:, both, :, :].rearrange("p q o t -> p (q o t)"),
-                )
+        def turn(n, g):
+            bank = psum_w.tile([P, 2, 2, P], F32, name="bank%d%d" % (n, g), tag="w_bank")
+            banks[n, g] = bank
+            words = w_raw[n][:].bitcast(F32)
+            for v in range(2):
+                for u in range(2):
+                    nc.tensor.transpose(
+                        bank[:, v, u, :], words[:, u::2, 2 * g + v], parted[:].rearrange("p s o -> p (s o)")
+                    )
 
-        def finish(r):
-            channels = slice(2 * r, 2 * r + 2)
+        def copy_out(n, g, engine_copy):
+            engine_copy(
+                out=w_grouped[:, 4 * g : 4 * g + 4, n * OH : (n + 1) * OH, :],
+                in_=banks[n, g][:].bitcast(BF16).rearrange("p w u (s o e) -> p w e o (u s)", s=2, e=2),
+            )
+
+        def quantise(w):
+            both = slice(2 * w, 2 * w + 2)
+            nc.vector.quantize_mx(
+                out=w_codes[:, both, :].rearrange("p q o -> p (q o)").bitcast(FP8X4),
+                scales=w_scales[:, both, :].rearrange("p q o -> p (q o)"),
+                in_=w_grouped[:, both, :, :].rearrange("p q o t -> p (q o t)"),
+            )
+
+        def multiply(r):
             acc = psum_acc.tile([P, 2, L], F32, tag="acc")
             for c in (2 * r, 2 * r + 1):
                 for k in range(KW):
@@ -121,6 +132,10 @@ def tile_timeawareconv1d_s_kernel(tc, x, time_tensor, weights, out):
                         start=(k == 0),
                         stop=(k == KW - 1),
                     )
+            return acc
+
+        def finish(r, acc):
+            channels = slice(2 * r, 2 * r + 2)
             nc.vector.tensor_tensor(
                 out=out_sb[:, channels, :].rearrange("p c (n e) -> p c n e", e=2),
                 in0=acc[:].rearrange("p c (e n) -> p c n e", e=2),
@@ -129,9 +144,22 @@ def tile_timeawareconv1d_s_kernel(tc, x, time_tensor, weights, out):
             )
             nc.sync.dma_start(out=out_rows[:, channels, :], in_=out_sb[:, channels, :])
 
-        copy_out(0)
-        quantise(0)
-        copy_out(1)
-        finish(0)
-        quantise(1)
-        finish(1)
+        for n in range(2):
+            for g in range(3):
+                turn(n, g)
+        copy_out(0, 0, nc.scalar.copy)
+        copy_out(0, 1, nc.vector.tensor_copy)
+        copy_out(0, 2, nc.scalar.copy)
+        nc.scalar.copy(out=time_all[:], in_=time_bank[:])
+        copy_out(1, 0, nc.scalar.copy)
+        copy_out(1, 1, nc.vector.tensor_copy)
+        copy_out(1, 2, nc.scalar.copy)
+        for w in range(3):
+            quantise(w)
+        acc0 = multiply(0)
+        quantise(3)
+        quantise(4)
+        finish(0, acc0)
+        quantise(5)
+        acc1 = multiply(1)
+        finish(1, acc1)

@@ -16,8 +16,10 @@ CK = C * KW
 PAIRS = CK // 2
 HALF = L // 2
 BLOCKS = KW + 1
-B32 = I // 32
-OH = O // 2
+CHUNKS = 4
+RAW = 2
+LATE = PAIRS - RAW
+PC = P // CHUNKS
 
 FLOPS = 2 * O * I * C * KW * L
 
@@ -25,9 +27,9 @@ FLOPS = 2 * O * I * C * KW * L
 def tile_timeawareconv1d_s_kernel(tc, x, time_tensor, weights, out):
     nc = tc.nc
 
-    x_rows = x.rearrange("a (b s r u) c l -> (a s) b r (u c l)", b=B32, s=2, r=8, u=2)
-    w_rows = weights.rearrange("(n o) (b s j) c k -> n s o b (j c k)", n=2, b=B32, s=2)
-    time_row = time_tensor.rearrange("b c l -> b (c l)")
+    x_rows = x.rearrange("b (p t) c l -> p (b t) (c l)", p=P)
+    w_rows = weights.rearrange("o i c k -> o (i c k)")
+    time_cols = time_tensor.rearrange("b c l -> (b c l)").rearrange("(p j) -> p j", p=P)
     out_rows = out.rearrange("b o c l -> o (b c) l")
 
     with ExitStack() as ctx:
@@ -36,50 +38,44 @@ def tile_timeawareconv1d_s_kernel(tc, x, time_tensor, weights, out):
         psum_acc = ctx.enter_context(tc.psum_pool(name="psum_acc", bufs=2))
         ctx.enter_context(tc.manual_schedule())
 
-        time_in_row0 = keep.tile([P, C * L], BF16)
-        nc.vector.memset(time_in_row0[:].bitcast(F32), 0.0)
-        nc.scalar.dma_start(out=time_in_row0[0:1, :], in_=time_row)
+        time_raw = keep.tile([P, C], BF16)
+        nc.scalar.dma_start(out=time_raw[:], in_=time_cols)
+        x_raw = keep.tile([P, PACK, C, L], BF16)
+        nc.sync.dma_start(out=x_raw[:].rearrange("p t c l -> p t (c l)"), in_=x_rows)
+        w_raw = keep.tile([P, I * CK], BF16)
+        chunk = I * CK // CHUNKS
+        for n in range(CHUNKS):
+            nc.sync.dma_start(out=w_raw[:, n * chunk : (n + 1) * chunk], in_=w_rows[:, n * chunk : (n + 1) * chunk])
 
-        x_raw = keep.tile([P, 2, 2, C, L], BF16)
-        w_raw = [keep.tile([P, B32 * 16, CK], BF16, name="w_raw%d" % n) for n in range(2)]
-        for s in range(2):
-            nc.sync.dma_start(
-                out=x_raw[:, s].rearrange("p u c l -> p (u c l)"),
-                in_=x_rows[s],
-            )
-        for n in range(2):
-            for s in range(2):
-                nc.sync.dma_start(
-                    out=w_raw[n][s::2].rearrange("o (b j) q -> o b (j q)", b=B32),
-                    in_=w_rows[n, s],
-                )
-
-        ones = keep.tile([P, P], BF16)
-        nc.vector.memset(ones[:], 1.0)
-
+        identity = keep.tile([P, P], F32)
+        make_identity(nc, identity[:])
+        identity_bf16 = keep.tile([P, P], BF16)
+        nc.vector.tensor_copy(out=identity_bf16[:], in_=identity[:])
         x_grouped = keep.tile([P, C, BLOCKS, HALF, PACK], BF16, align_bytes=64)
         x_codes = keep.tile([P, C, BLOCKS * HALF], U32, align_bytes=64)
         x_scales = keep.tile([P, C, BLOCKS * HALF], U8, align_bytes=64)
         nc.vector.memset(x_grouped[:, :, 0, 0, :], 0.0)
         nc.vector.memset(x_grouped[:, :, 3, HALF - 1, :], 0.0)
 
-        identity = keep.tile([P, P], F32)
-        make_identity(nc, identity[:])
-        parted = keep.tile([P, 2, OH], F32)
-        nc.vector.tensor_copy(out=parted[:], in_=identity[:].rearrange("p (o s) -> p s o", s=2))
-
         time_all = keep.tile([P, C, L], F32)
         time_bank = psum_acc.tile([P, C, L], F32, tag="acc")
-        nc.tensor.matmul(
-            out=time_bank[:].rearrange("p c l -> p (c l)"), lhsT=ones[:], rhs=time_in_row0[:], start=True, stop=True
+        for j in range(C):
+            nc.tensor.matmul(
+                out=time_bank[:, j, :],
+                lhsT=time_raw[:, j : j + 1].to_broadcast([P, P]),
+                rhs=identity_bf16[:],
+                start=True,
+                stop=True,
+            )
+        nc.scalar.copy(
+            out=time_all[:].rearrange("p c l -> p (c l)").rearrange("p (n j) -> p n j", j=C),
+            in_=time_bank[:].rearrange("p j n -> p n j"),
         )
 
-        x_by_parity = x_raw[:].rearrange("p s u c (n e) -> p e c n u s", e=2)
-        for blk in (1, 2):
-            nc.vector.tensor_copy(
-                out=x_grouped[:, :, blk, :, :].rearrange("p c n (u s) -> p c n u s", s=2), in_=x_by_parity[:, blk - 1]
-            )
-        nc.scalar.copy(out=x_grouped[:, :, 3, 0 : HALF - 1, :], in_=x_grouped[:, :, 1, 1:HALF, :])
+        x_by_parity = x_raw[:].rearrange("p t c (n e) -> p e c n t", e=2)
+        for block in (1, 2):
+            nc.vector.tensor_copy(out=x_grouped[:, :, block, :, :], in_=x_by_parity[:, block - 1])
+        nc.vector.tensor_copy(out=x_grouped[:, :, 3, 0 : HALF - 1, :], in_=x_grouped[:, :, 1, 1:HALF, :])
         nc.vector.tensor_copy(out=x_grouped[:, :, 0, 1:HALF, :], in_=x_grouped[:, :, 2, 0 : HALF - 1, :])
         nc.vector.quantize_mx(
             out=x_codes[:].rearrange("p c w -> p (c w)").bitcast(FP8X4),
@@ -92,23 +88,45 @@ def tile_timeawareconv1d_s_kernel(tc, x, time_tensor, weights, out):
         w_scales = keep.tile([P, CK, O], U8, align_bytes=64)
         out_sb = keep.tile([P, C, L], F32)
 
-        banks = {}
+        w_parted = keep.tile([P, 2 * LATE, 2, P, 2], BF16)
+        w_by_i = w_raw[:].rearrange("o (p u j q) -> o u p j q", u=2, j=2, q=CK)
+        for n in range(CHUNKS):
+            engine_copy = nc.scalar.copy if n < 2 else nc.vector.tensor_copy
+            rows = slice(n * PC, (n + 1) * PC)
+            for q in range(0, 2 * LATE, 4):
+                engine_copy(
+                    out=w_parted[:, q : q + 4, :, rows, :].rearrange("o q u p j -> o u p j q"),
+                    in_=w_by_i[:, :, rows, :, 2 * RAW + q : 2 * RAW + q + 4],
+                )
 
-        def turn(n, g):
-            bank = psum_w.tile([P, 2, 2, P], F32, name="bank%d%d" % (n, g), tag="w_bank")
-            banks[n, g] = bank
-            words = w_raw[n][:].bitcast(F32)
-            for v in range(2):
-                for u in range(2):
-                    nc.tensor.transpose(
-                        bank[:, v, u, :], words[:, u::2, 2 * g + v], parted[:].rearrange("p s o -> p (s o)")
-                    )
+        words = w_raw[:].bitcast(F32).rearrange("o (p t w) -> o p t w", t=PACK, w=PAIRS)
+        parted_words = w_parted[:].rearrange("o q u p j -> o (q u p j)").bitcast(F32)
+        banks = []
+        for w in range(PAIRS):
+            bank = psum_w.tile([P, PACK, O], F32, name="bank%d" % w, tag="w_bank")
+            banks.append(bank)
+            for t in range(PACK):
+                if w < RAW:
+                    columns = words[:, :, t, w]
+                else:
+                    start = ((w - RAW) * PACK + t) * P
+                    columns = parted_words[:, start : start + P]
+                nc.tensor.transpose(bank[:, t, :], columns, identity[:])
 
-        def copy_out(n, g, engine_copy):
-            engine_copy(
-                out=w_grouped[:, 4 * g : 4 * g + 4, n * OH : (n + 1) * OH, :],
-                in_=banks[n, g][:].bitcast(BF16).rearrange("p w u (s o e) -> p w e o (u s)", s=2, e=2),
-            )
+        def copy_out(w, engine_copy):
+            both = slice(2 * w, 2 * w + 2)
+            if w < RAW:
+                engine_copy(
+                    out=w_grouped[:, both, :, :],
+                    in_=banks[w][:].bitcast(BF16).rearrange("p t (o e) -> p e o t", e=2),
+                )
+            else:
+                engine_copy(
+                    out=w_grouped[:, both, :, :].rearrange("p q o t -> p (q o t)").bitcast(F32).rearrange(
+                        "p (q o u) -> p q o u", q=2, u=2
+                    ),
+                    in_=banks[w][:].rearrange("p (e u) o -> p e o u", u=2),
+                )
 
         def quantise(w):
             both = slice(2 * w, 2 * w + 2)
@@ -144,22 +162,14 @@ def tile_timeawareconv1d_s_kernel(tc, x, time_tensor, weights, out):
             )
             nc.sync.dma_start(out=out_rows[:, channels, :], in_=out_sb[:, channels, :])
 
-        for n in range(2):
-            for g in range(3):
-                turn(n, g)
-        copy_out(0, 0, nc.scalar.copy)
-        copy_out(0, 1, nc.vector.tensor_copy)
-        copy_out(0, 2, nc.scalar.copy)
-        nc.scalar.copy(out=time_all[:], in_=time_bank[:])
-        copy_out(1, 0, nc.scalar.copy)
-        copy_out(1, 1, nc.vector.tensor_copy)
-        copy_out(1, 2, nc.scalar.copy)
-        for w in range(3):
+        for w in (0, 2, 3, 4, 5):
+            copy_out(w, nc.scalar.copy)
+        copy_out(1, nc.vector.tensor_copy)
+        for w in range(4):
             quantise(w)
         acc0 = multiply(0)
-        quantise(3)
-        quantise(4)
         finish(0, acc0)
+        quantise(4)
         quantise(5)
         acc1 = multiply(1)
         finish(1, acc1)

@@ -49,32 +49,32 @@ def tile_timeawareconv1d_s_kernel(tc, x, time_tensor, weights, out):
 
         identity = keep.tile([P, P], F32)
         make_identity(nc, identity[:])
-        identity_bf16 = keep.tile([P, P], BF16)
-        nc.vector.tensor_copy(out=identity_bf16[:], in_=identity[:])
         x_grouped = keep.tile([P, C, BLOCKS, HALF, PACK], BF16, align_bytes=64)
         x_codes = keep.tile([P, C, BLOCKS * HALF], U32, align_bytes=64)
         x_scales = keep.tile([P, C, BLOCKS * HALF], U8, align_bytes=64)
         nc.vector.memset(x_grouped[:, :, 0, 0, :], 0.0)
         nc.vector.memset(x_grouped[:, :, 3, HALF - 1, :], 0.0)
 
+        time_f32 = keep.tile([P, C], F32)
         time_all = keep.tile([P, C, L], F32)
         time_bank = psum_acc.tile([P, C, L], F32, tag="acc")
-        for j in range(C):
-            nc.tensor.matmul(
-                out=time_bank[:, j, :],
-                lhsT=time_raw[:, j : j + 1].to_broadcast([P, P]),
-                rhs=identity_bf16[:],
-                start=True,
-                stop=True,
-            )
-        nc.scalar.copy(
-            out=time_all[:].rearrange("p c l -> p (c l)").rearrange("p (n j) -> p n j", j=C),
-            in_=time_bank[:].rearrange("p j n -> p n j"),
-        )
+
+        def spread_time():
+            nc.vector.tensor_copy(out=time_f32[:], in_=time_raw[:])
+            for j in range(C):
+                nc.tensor.matmul(
+                    out=time_bank[:, j, :],
+                    lhsT=time_f32[:, j : j + 1].to_broadcast([P, P]),
+                    rhs=identity[:],
+                    start=True,
+                    stop=True,
+                )
 
         x_by_parity = x_raw[:].rearrange("p t c (n e) -> p e c n t", e=2)
         for block in (1, 2):
             nc.vector.tensor_copy(out=x_grouped[:, :, block, :, :], in_=x_by_parity[:, block - 1])
+            if block == 1:
+                spread_time()
         nc.vector.tensor_copy(out=x_grouped[:, :, 3, 0 : HALF - 1, :], in_=x_grouped[:, :, 1, 1:HALF, :])
         nc.vector.tensor_copy(out=x_grouped[:, :, 0, 1:HALF, :], in_=x_grouped[:, :, 2, 0 : HALF - 1, :])
         nc.vector.quantize_mx(
@@ -98,6 +98,11 @@ def tile_timeawareconv1d_s_kernel(tc, x, time_tensor, weights, out):
                     out=w_parted[:, q : q + 4, :, rows, :].rearrange("o q u p j -> o u p j q"),
                     in_=w_by_i[:, :, rows, :, 2 * RAW + q : 2 * RAW + q + 4],
                 )
+
+        nc.scalar.copy(
+            out=time_all[:].rearrange("p c l -> p (c l)").rearrange("p (n j) -> p n j", j=C),
+            in_=time_bank[:].rearrange("p j n -> p n j"),
+        )
 
         words = w_raw[:].bitcast(F32).rearrange("o (p t w) -> o p t w", t=PACK, w=PAIRS)
         parted_words = w_parted[:].rearrange("o q u p j -> o (q u p j)").bitcast(F32)
@@ -168,8 +173,8 @@ def tile_timeawareconv1d_s_kernel(tc, x, time_tensor, weights, out):
         for w in range(4):
             quantise(w)
         acc0 = multiply(0)
-        finish(0, acc0)
         quantise(4)
         quantise(5)
+        finish(0, acc0)
         acc1 = multiply(1)
         finish(1, acc1)

@@ -17,8 +17,8 @@ PAIRS = CK // 2
 HALF = L // 2
 BLOCKS = KW + 1
 CHUNKS = 4
-RAW = 2
-LATE = PAIRS - RAW
+RAW = 1
+GROUPS = (slice(2, 6), slice(6, 10), slice(10, 12))
 PC = P // CHUNKS
 
 FLOPS = 2 * O * I * C * KW * L
@@ -88,18 +88,20 @@ def tile_timeawareconv1d_s_kernel(tc, x, time_tensor, weights, out):
         w_scales = keep.tile([P, CK, O], U8, align_bytes=64)
         out_sb = keep.tile([P, C, L], F32)
 
-        w_parted = keep.tile([P, 2 * LATE, 2, P, 2], BF16)
+        w_parted = keep.tile([P, CK, 2, P, 2], BF16)
         w_by_i = w_raw[:].rearrange("o (p u j q) -> o u p j q", u=2, j=2, q=CK)
-        for n in range(CHUNKS):
-            engine_copy = nc.scalar.copy if n < 2 else nc.vector.tensor_copy
-            rows = slice(n * PC, (n + 1) * PC)
-            for q in range(0, 2 * LATE, 4):
-                engine_copy(
-                    out=w_parted[:, q : q + 4, :, rows, :].rearrange("o q u p j -> o u p j q"),
-                    in_=w_by_i[:, :, rows, :, 2 * RAW + q : 2 * RAW + q + 4],
-                )
 
-        nc.scalar.copy(
+        def part(n, cks, engine_copy):
+            rows = slice(n * PC, (n + 1) * PC)
+            engine_copy(
+                out=w_parted[:, cks, :, rows, :].rearrange("o q u p j -> o u p j q"), in_=w_by_i[:, :, rows, :, cks]
+            )
+
+        for n in range(CHUNKS):
+            for cks in GROUPS:
+                part(n, cks, nc.vector.tensor_copy if n == CHUNKS - 1 or cks == GROUPS[2] else nc.scalar.copy)
+
+        nc.vector.tensor_copy(
             out=time_all[:].rearrange("p c l -> p (c l)").rearrange("p (n j) -> p n j", j=C),
             in_=time_bank[:].rearrange("p j n -> p n j"),
         )
@@ -114,7 +116,7 @@ def tile_timeawareconv1d_s_kernel(tc, x, time_tensor, weights, out):
                 if w < RAW:
                     columns = words[:, :, t, w]
                 else:
-                    start = ((w - RAW) * PACK + t) * P
+                    start = (w * PACK + t) * P
                     columns = parted_words[:, start : start + P]
                 nc.tensor.transpose(bank[:, t, :], columns, identity[:])
 

@@ -77,12 +77,6 @@ def tile_timeawareconv1d_s_kernel(tc, x, time_tensor, weights, out):
                 spread_time()
         nc.vector.tensor_copy(out=x_grouped[:, :, 3, 0 : HALF - 1, :], in_=x_grouped[:, :, 1, 1:HALF, :])
         nc.vector.tensor_copy(out=x_grouped[:, :, 0, 1:HALF, :], in_=x_grouped[:, :, 2, 0 : HALF - 1, :])
-        nc.vector.quantize_mx(
-            out=x_codes[:].rearrange("p c w -> p (c w)").bitcast(FP8X4),
-            scales=x_scales[:].rearrange("p c w -> p (c w)"),
-            in_=x_grouped[:].rearrange("p c s n t -> p (c s n t)"),
-        )
-
         w_grouped = keep.tile([P, CK, O, PACK], BF16, align_bytes=64)
         w_codes = keep.tile([P, CK, O], U32, align_bytes=64)
         w_scales = keep.tile([P, CK, O], U8, align_bytes=64)
@@ -97,8 +91,16 @@ def tile_timeawareconv1d_s_kernel(tc, x, time_tensor, weights, out):
                 out=w_parted[:, cks, :, rows, :].rearrange("o q u p j -> o u p j q"), in_=w_by_i[:, :, rows, :, cks]
             )
 
+        part(0, GROUPS[2], nc.vector.tensor_copy)
+        nc.vector.quantize_mx(
+            out=x_codes[:].rearrange("p c w -> p (c w)").bitcast(FP8X4),
+            scales=x_scales[:].rearrange("p c w -> p (c w)"),
+            in_=x_grouped[:].rearrange("p c s n t -> p (c s n t)"),
+        )
         for n in range(CHUNKS):
             for cks in GROUPS:
+                if n == 0 and cks == GROUPS[2]:
+                    continue
                 part(n, cks, nc.vector.tensor_copy if n == CHUNKS - 1 or cks == GROUPS[2] else nc.scalar.copy)
 
         nc.vector.tensor_copy(
@@ -143,40 +145,47 @@ def tile_timeawareconv1d_s_kernel(tc, x, time_tensor, weights, out):
                 in_=w_grouped[:, both, :, :].rearrange("p q o t -> p (q o t)"),
             )
 
-        def multiply(r):
-            acc = psum_acc.tile([P, 2, L], F32, tag="acc")
-            for c in (2 * r, 2 * r + 1):
-                for k in range(KW):
-                    window = slice(k * HALF, k * HALF + L)
-                    nc.tensor.matmul_mx(
-                        out=acc[:, c % 2, :],
-                        lhsT=w_codes[:, c * KW + k, :].bitcast(FP8X4),
-                        lhsT_scale=w_scales[:, c * KW + k, :],
-                        rhs=x_codes[:, c, window].bitcast(FP8X4),
-                        rhs_scale=x_scales[:, c, window],
-                        start=(k == 0),
-                        stop=(k == KW - 1),
-                    )
-            return acc
+        def multiply(c, out):
+            for k in range(KW):
+                window = slice(k * HALF, k * HALF + L)
+                nc.tensor.matmul_mx(
+                    out=out,
+                    lhsT=w_codes[:, c * KW + k, :].bitcast(FP8X4),
+                    lhsT_scale=w_scales[:, c * KW + k, :],
+                    rhs=x_codes[:, c, window].bitcast(FP8X4),
+                    rhs_scale=x_scales[:, c, window],
+                    start=(k == 0),
+                    stop=(k == KW - 1),
+                )
 
-        def finish(r, acc):
-            channels = slice(2 * r, 2 * r + 2)
+        def finish(channels, acc):
             nc.vector.tensor_tensor(
                 out=out_sb[:, channels, :].rearrange("p c (n e) -> p c n e", e=2),
-                in0=acc[:].rearrange("p c (e n) -> p c n e", e=2),
+                in0=acc.rearrange("p c (e n) -> p c n e", e=2),
                 in1=time_all[:, channels, :].rearrange("p c (n e) -> p c n e", e=2),
                 op=mybir.AluOpType.mult,
             )
+
+        def store(channels):
             nc.sync.dma_start(out=out_rows[:, channels, :], in_=out_sb[:, channels, :])
 
-        for w in (0, 2, 3, 4, 5):
+        for w in (0, 2, 4, 5):
             copy_out(w, nc.scalar.copy)
-        copy_out(1, nc.vector.tensor_copy)
+        for w in (1, 3):
+            copy_out(w, nc.vector.tensor_copy)
         for w in range(4):
             quantise(w)
-        acc0 = multiply(0)
+        acc01 = psum_acc.tile([P, 2, L], F32, name="acc01", tag="acc")
+        acc2 = psum_acc.tile([P, 1, L], F32, name="acc2", tag="acc")
+        acc3 = psum_w.tile([P, 1, L], F32, name="acc3", tag="w_bank")
+        multiply(0, acc01[:, 0, :])
+        multiply(1, acc01[:, 1, :])
         quantise(4)
+        multiply(2, acc2[:, 0, :])
         quantise(5)
-        finish(0, acc0)
-        acc1 = multiply(1)
-        finish(1, acc1)
+        multiply(3, acc3[:, 0, :])
+        finish(slice(0, 2), acc01[:])
+        finish(slice(2, 3), acc2[:])
+        store(slice(0, 3))
+        finish(slice(3, 4), acc3[:])
+        store(slice(3, 4))

from contextlib import ExitStack

import concourse.mybir as mybir
from concourse.masks import make_identity

BF16 = mybir.dt.bfloat16
F32 = mybir.dt.float32
U32 = mybir.dt.uint32
U8 = mybir.dt.uint8
FP8X4 = mybir.dt.float8_e4m3fn_x4

P = 128
PACK = 4
I, C, L, O, KW = 512, 4, 128, 128, 3
CK = C * KW
PAIRS = CK // 2
HALF = L // 2
BLOCKS = KW + 1
CHUNKS = 4
RAW = 1
GROUPS = (slice(2, 6), slice(6, 10), slice(10, 12))
PC = P // CHUNKS

FLOPS = 2 * O * I * C * KW * L


def tile_timeawareconv1d_s_kernel(tc, x, time_tensor, weights, out):
    nc = tc.nc

    x_rows = x.rearrange("b (p t) c l -> p (b t) (c l)", p=P)
    w_rows = weights.rearrange("o i c k -> o (i c k)")
    time_cols = time_tensor.rearrange("b c l -> (b c l)").rearrange("(p j) -> p j", p=P)
    out_rows = out.rearrange("b o c l -> o (b c) l")

    with ExitStack() as ctx:
        keep = ctx.enter_context(tc.tile_pool(name="keep", bufs=1))
        psum_w = ctx.enter_context(tc.psum_pool(name="psum_w", bufs=6))
        psum_acc = ctx.enter_context(tc.psum_pool(name="psum_acc", bufs=2))
        ctx.enter_context(tc.manual_schedule())

        time_raw = keep.tile([P, C], BF16)
        nc.scalar.dma_start(out=time_raw[:], in_=time_cols)
        x_raw = keep.tile([P, PACK, C, L], BF16)
        nc.sync.dma_start(out=x_raw[:].rearrange("p t c l -> p t (c l)"), in_=x_rows)
        w_raw = keep.tile([P, I * CK], BF16)
        chunk = I * CK // CHUNKS
        for n in range(CHUNKS):
            nc.sync.dma_start(out=w_raw[:, n * chunk : (n + 1) * chunk], in_=w_rows[:, n * chunk : (n + 1) * chunk])

        identity = keep.tile([P, P], F32)
        make_identity(nc, identity[:])
        x_grouped = keep.tile([P, C, BLOCKS, HALF, PACK], BF16, align_bytes=64)
        x_codes = keep.tile([P, C, BLOCKS * HALF], U32, align_bytes=64)
        x_scales = keep.tile([P, C, BLOCKS * HALF], U8, align_bytes=64)
        nc.vector.memset(x_grouped[:, :, 0, 0, :], 0.0)
        nc.vector.memset(x_grouped[:, :, 3, HALF - 1, :], 0.0)

        time_f32 = keep.tile([P, C], F32)
        time_all = keep.tile([P, C, L], F32)
        time_bank = psum_acc.tile([P, C, L], F32, tag="acc")

        def spread_time():
            nc.vector.tensor_copy(out=time_f32[:], in_=time_raw[:])
            for j in range(C):
                nc.tensor.matmul(
                    out=time_bank[:, j, :],
                    lhsT=time_f32[:, j : j + 1].to_broadcast([P, P]),
                    rhs=identity[:],
                    start=True,
                    stop=True,
                )

        x_by_parity = x_raw[:].rearrange("p t c (n e) -> p e c n t", e=2)
        for block in (1, 2):
            nc.vector.tensor_copy(out=x_grouped[:, :, block, :, :], in_=x_by_parity[:, block - 1])
            if block == 1:
                spread_time()
        nc.vector.tensor_copy(out=x_grouped[:, :, 3, 0 : HALF - 1, :], in_=x_grouped[:, :, 1, 1:HALF, :])
        nc.vector.tensor_copy(out=x_grouped[:, :, 0, 1:HALF, :], in_=x_grouped[:, :, 2, 0 : HALF - 1, :])
        w_grouped = keep.tile([P, CK, O, PACK], BF16, align_bytes=64)
        w_codes = keep.tile([P, CK, O], U32, align_bytes=64)
        w_scales = keep.tile([P, CK, O], U8, align_bytes=64)
        out_sb = keep.tile([P, C, L], F32)

        w_parted = keep.tile([P, CK, 2, P, 2], BF16)
        w_by_i = w_raw[:].rearrange("o (p u j q) -> o u p j q", u=2, j=2, q=CK)

        def part(n, cks, engine_copy):
            rows = slice(n * PC, (n + 1) * PC)
            engine_copy(
                out=w_parted[:, cks, :, rows, :].rearrange("o q u p j -> o u p j q"), in_=w_by_i[:, :, rows, :, cks]
            )

        part(0, GROUPS[2], nc.vector.tensor_copy)
        nc.vector.quantize_mx(
            out=x_codes[:].rearrange("p c w -> p (c w)").bitcast(FP8X4),
            scales=x_scales[:].rearrange("p c w -> p (c w)"),
            in_=x_grouped[:].rearrange("p c s n t -> p (c s n t)"),
        )
        for n in range(CHUNKS):
            for cks in GROUPS:
                if n == 0 and cks == GROUPS[2]:
                    continue
                part(n, cks, nc.vector.tensor_copy if n == CHUNKS - 1 or cks == GROUPS[2] else nc.scalar.copy)

        nc.vector.tensor_copy(
            out=time_all[:].rearrange("p c l -> p (c l)").rearrange("p (n j) -> p n j", j=C),
            in_=time_bank[:].rearrange("p j n -> p n j"),
        )

        words = w_raw[:].bitcast(F32).rearrange("o (p t w) -> o p t w", t=PACK, w=PAIRS)
        parted_words = w_parted[:].rearrange("o q u p j -> o (q u p j)").bitcast(F32)
        banks = []
        for w in range(PAIRS):
            bank = psum_w.tile([P, PACK, O], F32, name="bank%d" % w, tag="w_bank")
            banks.append(bank)
            for t in range(PACK):
                if w < RAW:
                    columns = words[:, :, t, w]
                else:
                    start = (w * PACK + t) * P
                    columns = parted_words[:, start : start + P]
                nc.tensor.transpose(bank[:, t, :], columns, identity[:])

        def copy_out(w, engine_copy):
            both = slice(2 * w, 2 * w + 2)
            if w < RAW:
                engine_copy(
                    out=w_grouped[:, both, :, :],
                    in_=banks[w][:].bitcast(BF16).rearrange("p t (o e) -> p e o t", e=2),
                )
            else:
                engine_copy(
                    out=w_grouped[:, both, :, :].rearrange("p q o t -> p (q o t)").bitcast(F32).rearrange(
                        "p (q o u) -> p q o u", q=2, u=2
                    ),
                    in_=banks[w][:].rearrange("p (e u) o -> p e o u", u=2),
                )

        def quantise(w):
            both = slice(2 * w, 2 * w + 2)
            nc.vector.quantize_mx(
                out=w_codes[:, both, :].rearrange("p q o -> p (q o)").bitcast(FP8X4),
                scales=w_scales[:, both, :].rearrange("p q o -> p (q o)"),
                in_=w_grouped[:, both, :, :].rearrange("p q o t -> p (q o t)"),
            )

        def multiply(c, out):
            for k in range(KW):
                window = slice(k * HALF, k * HALF + L)
                nc.tensor.matmul_mx(
                    out=out,
                    lhsT=w_codes[:, c * KW + k, :].bitcast(FP8X4),
                    lhsT_scale=w_scales[:, c * KW + k, :],
                    rhs=x_codes[:, c, window].bitcast(FP8X4),
                    rhs_scale=x_scales[:, c, window],
                    start=(k == 0),
                    stop=(k == KW - 1),
                )

        def finish(channels, acc):
            nc.vector.tensor_tensor(
                out=out_sb[:, channels, :].rearrange("p c (n e) -> p c n e", e=2),
                in0=acc.rearrange("p c (e n) -> p c n e", e=2),
                in1=time_all[:, channels, :].rearrange("p c (n e) -> p c n e", e=2),
                op=mybir.AluOpType.mult,
            )

        def store(channels):
            nc.sync.dma_start(out=out_rows[:, channels, :], in_=out_sb[:, channels, :])

        for w in (0, 2, 4, 5):
            copy_out(w, nc.scalar.copy)
        for w in (1, 3):
            copy_out(w, nc.vector.tensor_copy)
        for w in range(4):
            quantise(w)
        acc01 = psum_acc.tile([P, 2, L], F32, name="acc01", tag="acc")
        acc2 = psum_acc.tile([P, 1, L], F32, name="acc2", tag="acc")
        acc3 = psum_w.tile([P, 1, L], F32, name="acc3", tag="w_bank")
        multiply(0, acc01[:, 0, :])
        multiply(1, acc01[:, 1, :])
        quantise(4)
        multiply(2, acc2[:, 0, :])
        quantise(5)
        multiply(3, acc3[:, 0, :])
        finish(slice(0, 2), acc01[:])
        finish(slice(2, 3), acc2[:])
        store(slice(0, 3))
        finish(slice(3, 4), acc3[:])
        store(slice(3, 4))
